import numpy as np
import ml_dtypes


def mxq(x, axis, fmt="e4m3"):
    dtype, down = {"e4m3": (ml_dtypes.float8_e4m3fn, 7), "e5m2": (ml_dtypes.float8_e5m2, 14)}[fmt]
    v = np.moveaxis(np.asarray(x, np.float32).astype(ml_dtypes.bfloat16).astype(np.float64), axis, -1)
    blocks = v.reshape(v.shape[:-1] + (-1, 32))
    amax = np.abs(blocks).max(-1, keepdims=True)
    byte = np.maximum(np.where(amax > 0, np.frexp(amax)[1] - 1 + 127, 0) - down, 1)
    scale = np.exp2(byte - 127.0)
    codes = (blocks / scale).astype(np.float32).astype(dtype).astype(np.float64)
    return np.moveaxis((codes * scale).reshape(v.shape), -1, axis)


WIDE = False


def mx_kscale(k):
    if not WIDE:
        return np.ones(k)
    levels = np.array([10, -10, 5, -5, 0])
    a = np.random.permutation(np.resize(levels, k // 512 * 4)).reshape(k // 512, 4)
    idx = np.arange(k)
    return np.exp2(a[idx // 512, idx % 128 // 32])


BF16 = ml_dtypes.bfloat16


def bf(x):
    return np.asarray(x, np.float32).astype(BF16)


def f64(x):
    return np.asarray(x).astype(np.float64)


B, D, N, K = 4, 512, 4096, 128
EPS = 1e-06


def setup_inputs():
    t = np.exp2(np.round(np.log2(mx_kscale(D)) / 2))[None, :, None]
    r = np.sqrt(D)
    x = (10.0 * np.random.standard_normal((B, D, N)) + 6.0 * np.random.standard_normal((B, D, 1))) / r
    mu = 3.5 * np.random.standard_normal((1, D, K)) / r
    sigma = 1.0 + 9.0 / r * (np.random.random((1, D, K)) - 0.5)
    return {"x": bf(x * t), "mu": bf(mu * t), "sigma": bf(sigma * t), "alpha": bf(3.0 + 0.1 * np.random.standard_normal(1))}


def reference(x, mu, sigma, alpha):
    x = f64(x)
    mu_dk = f64(mu)[0]
    sigma_c = np.maximum(f64(sigma)[0], EPS)
    inv_s2 = 1.0 / (sigma_c * sigma_c)
    x2 = x * x
    t_x2 = mxq(inv_s2, 0, "e4m3").T @ mxq(x2, 1, "e4m3")
    t_xm = mxq(mu_dk * inv_s2, 0, "e4m3").T @ mxq(x, 1, "e4m3")
    t_m2 = np.sum(mu_dk * mu_dk * inv_s2, axis=0)
    dist = t_x2 - 2.0 * t_xm + t_m2[None, :, None]
    log_det = np.sum(np.log(sigma_c), axis=0)
    logits = -0.5 * dist - log_det[None, :, None] + f64(alpha)[0]
    e = np.exp(logits - logits.max(axis=1, keepdims=True))
    return e / e.sum(axis=1, keepdims=True)

@@ -1,0 +1,227 @@
+import concourse.mybir as mybir
+from concourse.masks import make_identity
+
+F32 = mybir.dt.float32
+BF16 = mybir.dt.bfloat16
+U32 = mybir.dt.uint32
+U8 = mybir.dt.uint8
+FP8X4 = mybir.dt.float8_e4m3fn_x4
+ALU = mybir.AluOpType
+ACT = mybir.ActivationFunctionType
+AXIS = mybir.AxisListType
+
+B, D, N, K = 4, 512, 4096, 128
+EPS = 1e-06
+P = 128
+PACK = 4
+UNIT = 512
+BLOCKS = UNIT // P
+UNITS_PER_BATCH = N // UNIT
+UNITS = B * UNITS_PER_BATCH
+SQUARE_LEAD = 6
+LOADS_AHEAD = SQUARE_LEAD + 2
+LAST_STEP_LAG = 5
+SCALAR_SQUARE_POINTS = 384
+
+FLOPS = 2 * 2 * B * D * K * N
+
+
+def prepare_clusters(nc, const, psum, mu, sigma, ident):
+    sig_raw = const.tile([P, PACK, K], BF16)
+    mu_raw = const.tile([P, PACK, K], BF16)
+    nc.scalar.dma_start(out=sig_raw[:], in_=sigma.flatten_outer_dims().rearrange("(p j) k -> p j k", j=PACK))
+    nc.scalar.dma_start(out=mu_raw[:], in_=mu.flatten_outer_dims().rearrange("(p j) k -> p j k", j=PACK))
+
+    sc = const.tile([P, PACK, K], F32)
+    nc.vector.tensor_scalar_max(out=sc[:], in0=sig_raw[:], scalar1=EPS)
+    log_sc = const.tile([P, PACK, K], F32)
+    nc.scalar.activation(out=log_sc[:], in_=sc[:], func=ACT.Ln)
+    inv_s2 = const.tile([P, PACK, K], F32)
+    nc.vector.tensor_mul(out=inv_s2[:], in0=sc[:], in1=sc[:])
+    nc.vector.reciprocal(out=inv_s2[:], in_=inv_s2[:])
+    mu_inv = const.tile([P, PACK, K], F32)
+    nc.vector.tensor_mul(out=mu_inv[:], in0=mu_raw[:], in1=inv_s2[:])
+
+    w_grouped = const.tile([P, 2, K, PACK], BF16, align_bytes=64)
+    nc.vector.tensor_scalar_mul(out=w_grouped[:, 0], in0=inv_s2[:].rearrange("p j k -> p k j"), scalar1=-0.5)
+    nc.vector.tensor_copy(out=w_grouped[:, 1], in_=mu_inv[:].rearrange("p j k -> p k j"))
+    w_codes = const.tile([P, 2, K], U32, align_bytes=64)
+    w_scales = const.tile([P, 2, K], U8, align_bytes=64)
+    nc.vector.quantize_mx(
+        out=w_codes[:].rearrange("p w k -> p (w k)").bitcast(FP8X4),
+        scales=w_scales[:].rearrange("p w k -> p (w k)"),
+        in_=w_grouped[:].rearrange("p w k j -> p (w k j)"),
+    )
+
+    term = const.tile([P, PACK, K], F32)
+    nc.vector.tensor_mul(out=term[:], in0=mu_raw[:], in1=mu_inv[:])
+    nc.vector.scalar_tensor_tensor(
+        out=term[:], in0=term[:], scalar=-0.5, in1=log_sc[:], op0=ALU.mult, op1=ALU.subtract
+    )
+    term_t = psum.tile([P, PACK, P], F32, tag="by_point", bufs=3)
+    for j in range(PACK):
+        nc.tensor.transpose(term_t[:, j, :], term[:, j, :], ident[:])
+    bias = const.tile([P, 1], F32)
+    nc.vector.tensor_reduce(out=bias[:], in_=term_t[:], axis=AXIS.XY, op=ALU.add)
+    return w_codes, w_scales, bias
+
+
+def tile_wassvladlayer_pa_kernel(tc, x, mu, sigma, alpha, out):
+    nc = tc.nc
+    with (
+        tc.tile_pool(name="const", bufs=1) as const,
+        tc.tile_pool(name="load", bufs=LOADS_AHEAD + 2) as load,
+        tc.tile_pool(name="squares", bufs=SQUARE_LEAD + 2) as squares,
+        tc.tile_pool(name="work", bufs=2) as work,
+        tc.tile_pool(name="store", bufs=3) as store,
+        tc.psum_pool(name="psum", bufs=2) as psum,
+        tc.manual_schedule(),
+    ):
+        held = {}
+        cut = SCALAR_SQUARE_POINTS
+
+        def is_unit(u):
+            return 0 <= u < UNITS
+
+        def hbm_cols(u):
+            first = (u % UNITS_PER_BATCH) * UNIT
+            return u // UNITS_PER_BATCH, slice(first, first + UNIT)
+
+        def load_x(u):
+            if not is_unit(u):
+                return
+            b, cols = hbm_cols(u)
+            raw = load.tile([P, PACK, UNIT], BF16)
+            nc.sync.dma_start(out=raw[:], in_=x[b, :, cols].rearrange("(p j) n -> p j n", j=PACK))
+            held["raw", u] = raw
+
+        def group_x(u):
+            if not is_unit(u):
+                return
+            x_grouped = work.tile([P, UNIT, PACK], BF16, align_bytes=64)
+            nc.vector.tensor_copy(
+                out=x_grouped[:].rearrange("p (c i) j -> p c j i", i=4),
+                in_=held["raw", u][:].rearrange("p j (c i) -> p c j i", i=4),
+            )
+            held["x", u] = x_grouped[:].rearrange("p n j -> p (n j)")
+
+        def square_on_scalar(u):
+            if not is_unit(u):
+                return
+            sq_grouped = squares.tile([P, UNIT, PACK], BF16, align_bytes=64)
+            nc.scalar.activation(
+                out=sq_grouped[:, :cut, :].rearrange("p (c i) j -> p c j i", i=4),
+                in_=held["raw", u][:, :, :cut].rearrange("p j (c i) -> p c j i", i=4),
+                func=ACT.Square,
+            )
+            held["sq", u] = sq_grouped[:].rearrange("p n j -> p (n j)")
+
+        def square_on_vector(u):
+            if not is_unit(u):
+                return
+            rest = slice(cut * PACK, UNIT * PACK)
+            nc.vector.tensor_mul(out=held["sq", u][:, rest], in0=held["x", u][:, rest], in1=held["x", u][:, rest])
+
+        def quantise(what, u):
+            if not is_unit(u):
+                return
+            codes = work.tile([P, UNIT], U32, align_bytes=64, tag=what + "_codes")
+            scales = work.tile([P, UNIT], U8, align_bytes=64, tag=what + "_scales")
+            nc.vector.quantize_mx(out=codes[:].bitcast(FP8X4), scales=scales[:], in_=held[what, u][:])
+            held[what + "_mx", u] = (codes, scales)
+
+        def multiply(u):
+            if not is_unit(u):
+                return
+            acc = psum.tile([P, UNIT], F32, tag="by_cluster")
+            for w, what in enumerate(("sq_mx", "x_mx")):
+                codes, scales = held[what, u]
+                nc.tensor.matmul_mx(
+                    out=acc[:],
+                    lhsT=w_codes[:, w, :].bitcast(FP8X4),
+                    lhsT_scale=w_scales[:, w, :],
+                    rhs=codes[:].bitcast(FP8X4),
+                    rhs_scale=scales[:],
+                    start=(w == 0),
+                    stop=(w == 1),
+                )
+            held["acc", u] = acc
+
+        def add_bias_and_transpose(u):
+            if not is_unit(u):
+                return
+            logits = work.tile([P, BLOCKS, P], F32)
+            nc.scalar.activation(
+                out=logits[:].rearrange("k g n -> k (g n)"), in_=held["acc", u][:], func=ACT.Identity, bias=bias[:, 0:1]
+            )
+            logits_t = psum.tile([P, BLOCKS, P], F32, tag="by_point", bufs=3)
+            for g in range(BLOCKS):
+                nc.tensor.transpose(logits_t[:, g, :], logits[:, g, :], ident[:])
+            held["logits_t", u] = logits_t
+
+        def find_max(u):
+            if not is_unit(u):
+                return
+            neg_max = work.tile([P, BLOCKS], F32)
+            nc.vector.tensor_reduce(out=neg_max[:], in_=held["logits_t", u][:], axis=AXIS.X, op=ALU.max, negate=True)
+            held["neg_max", u] = neg_max
+
+        def exponentiate(u):
+            if not is_unit(u):
+                return
+            expo = work.tile([P, BLOCKS, P], F32)
+            total = work.tile([P, BLOCKS], F32)
+            for g in range(BLOCKS):
+                nc.scalar.activation(
+                    out=expo[:, g, :],
+                    in_=held["logits_t", u][:, g, :],
+                    func=ACT.Exp,
+                    bias=held["neg_max", u][:, g : g + 1],
+                    accum_out=total[:, g : g + 1],
+                )
+            held["expo", u] = (expo, total)
+
+        def normalise_and_transpose(u):
+            if not is_unit(u):
+                return
+            expo, total = held["expo", u]
+            inv_total = work.tile([P, BLOCKS], F32)
+            nc.vector.reciprocal(out=inv_total[:], in_=total[:])
+            prob = work.tile([P, BLOCKS, P], F32)
+            for g in range(BLOCKS):
+                nc.vector.tensor_scalar_mul(out=prob[:, g, :], in0=expo[:, g, :], scalar1=inv_total[:, g : g + 1])
+            prob_t = psum.tile([P, BLOCKS, P], F32, tag="back")
+            for g in range(BLOCKS):
+                nc.tensor.transpose(prob_t[:, g, :], prob[:, g, :], ident[:])
+            held["prob_t", u] = prob_t
+
+        def store_out(u):
+            if not is_unit(u):
+                return
+            b, cols = hbm_cols(u)
+            result = store.tile([P, UNIT], F32)
+            nc.scalar.copy(out=result[:], in_=held["prob_t", u][:].rearrange("k g n -> k (g n)"))
+            nc.sync.dma_start(out=out[b, :, cols], in_=result[:])
+
+        ident = const.tile([P, P], F32)
+        make_identity(nc, ident[:])
+        w_codes, w_scales, bias = prepare_clusters(nc, const, psum, mu, sigma, ident)
+        for u in range(LOADS_AHEAD):
+            load_x(u)
+        for u in range(SQUARE_LEAD):
+            square_on_scalar(u)
+        group_x(0)
+
+        for i in range(UNITS + LAST_STEP_LAG):
+            load_x(i + LOADS_AHEAD)
+            quantise("sq", i - 1)
+            multiply(i - 1)
+            square_on_scalar(i + SQUARE_LEAD)
+            quantise("x", i)
+            square_on_vector(i)
+            add_bias_and_transpose(i - 1)
+            find_max(i - 2)
+            exponentiate(i - 3)
+            group_x(i + 1)
+            store_out(i - LAST_STEP_LAG)
+            normalise_and_transpose(i - 4)

@@ -21,7 +21,7 @@ UNITS = B * UNITS_PER_BATCH
 SQUARE_LEAD = 6
 LOADS_AHEAD = SQUARE_LEAD + 2
 LAST_STEP_LAG = 5
-SCALAR_SQUARE_POINTS = 384
+SCALAR_SQUARE_POINTS = 320
 
 FLOPS = 2 * 2 * B * D * K * N
 

@@ -18,33 +18,42 @@ UNIT = 512
 BLOCKS = UNIT // P
 UNITS_PER_BATCH = N // UNIT
 UNITS = B * UNITS_PER_BATCH
-SQUARE_LEAD = 6
-LOADS_AHEAD = SQUARE_LEAD + 2
-LAST_STEP_LAG = 5
-SCALAR_SQUARE_POINTS = 320
+LOADS_AHEAD = 3
+LAST_STEP_LAG = 4
+SCALAR_SQUARE_POINTS = 384
 
 FLOPS = 2 * 2 * B * D * K * N
 
 
-def prepare_clusters(nc, const, psum, mu, sigma, ident):
+def start_clusters(nc, const, mu, sigma):
     sig_raw = const.tile([P, PACK, K], BF16)
     mu_raw = const.tile([P, PACK, K], BF16)
     nc.scalar.dma_start(out=sig_raw[:], in_=sigma.flatten_outer_dims().rearrange("(p j) k -> p j k", j=PACK))
     nc.scalar.dma_start(out=mu_raw[:], in_=mu.flatten_outer_dims().rearrange("(p j) k -> p j k", j=PACK))
-
     sc = const.tile([P, PACK, K], F32)
     nc.vector.tensor_scalar_max(out=sc[:], in0=sig_raw[:], scalar1=EPS)
     log_sc = const.tile([P, PACK, K], F32)
     nc.scalar.activation(out=log_sc[:], in_=sc[:], func=ACT.Ln)
+    s2 = const.tile([P, PACK, K], F32)
+    nc.scalar.activation(out=s2[:], in_=sc[:], func=ACT.Square)
+    estimate = const.tile([P, PACK, K], F32)
+    nc.scalar.activation(out=estimate[:], in_=log_sc[:], func=ACT.Exp, scale=-2.0)
+    return mu_raw, log_sc, s2, estimate
+
+
+def finish_clusters(nc, const, psum, ident, mu_raw, log_sc, s2, estimate):
     inv_s2 = const.tile([P, PACK, K], F32)
-    nc.vector.tensor_mul(out=inv_s2[:], in0=sc[:], in1=sc[:])
-    nc.vector.reciprocal(out=inv_s2[:], in_=inv_s2[:])
+    nc.vector.tensor_mul(out=inv_s2[:], in0=s2[:], in1=estimate[:])
+    nc.vector.tensor_scalar(out=inv_s2[:], in0=inv_s2[:], scalar1=-1.0, scalar2=2.0, op0=ALU.mult, op1=ALU.add)
+    nc.vector.tensor_mul(out=inv_s2[:], in0=inv_s2[:], in1=estimate[:])
     mu_inv = const.tile([P, PACK, K], F32)
     nc.vector.tensor_mul(out=mu_inv[:], in0=mu_raw[:], in1=inv_s2[:])
+    mu2_inv = const.tile([P, PACK, K], F32)
+    nc.vector.tensor_mul(out=mu2_inv[:], in0=mu_raw[:], in1=mu_inv[:])
 
     w_grouped = const.tile([P, 2, K, PACK], BF16, align_bytes=64)
-    nc.vector.tensor_scalar_mul(out=w_grouped[:, 0], in0=inv_s2[:].rearrange("p j k -> p k j"), scalar1=-0.5)
-    nc.vector.tensor_copy(out=w_grouped[:, 1], in_=mu_inv[:].rearrange("p j k -> p k j"))
+    nc.scalar.activation(out=w_grouped[:, 0], in_=inv_s2[:].rearrange("p j k -> p k j"), func=ACT.Copy, scale=-0.5)
+    nc.scalar.copy(out=w_grouped[:, 1], in_=mu_inv[:].rearrange("p j k -> p k j"))
     w_codes = const.tile([P, 2, K], U32, align_bytes=64)
     w_scales = const.tile([P, 2, K], U8, align_bytes=64)
     nc.vector.quantize_mx(
@@ -53,16 +62,21 @@ def prepare_clusters(nc, const, psum, mu, sigma, ident):
         in_=w_grouped[:].rearrange("p w k j -> p (w k j)"),
     )
 
-    term = const.tile([P, PACK, K], F32)
-    nc.vector.tensor_mul(out=term[:], in0=mu_raw[:], in1=mu_inv[:])
-    nc.vector.scalar_tensor_tensor(
-        out=term[:], in0=term[:], scalar=-0.5, in1=log_sc[:], op0=ALU.mult, op1=ALU.subtract
-    )
-    term_t = psum.tile([P, PACK, P], F32, tag="by_point", bufs=3)
-    for j in range(PACK):
-        nc.tensor.transpose(term_t[:, j, :], term[:, j, :], ident[:])
+    sums = const.tile([P, 2], F32)
+    unread = const.tile([P, 2, PACK * P], F32)
+    for t, (term, factor, tag) in enumerate(((mu2_inv, -0.5, "by_point"), (log_sc, -1.0, "back"))):
+        term_t = psum.tile([P, PACK, P], F32, tag=tag)
+        for j in range(PACK):
+            nc.tensor.transpose(term_t[:, j, :], term[:, j, :], ident[:])
+        nc.scalar.activation(
+            out=unread[:, t, :],
+            in_=term_t[:].rearrange("k j p -> k (j p)"),
+            func=ACT.Copy,
+            scale=factor,
+            accum_out=sums[:, t : t + 1],
+        )
     bias = const.tile([P, 1], F32)
-    nc.vector.tensor_reduce(out=bias[:], in_=term_t[:], axis=AXIS.XY, op=ALU.add)
+    nc.vector.tensor_add(out=bias[:], in0=sums[:, 0:1], in1=sums[:, 1:2])
     return w_codes, w_scales, bias
 
 
@@ -71,7 +85,6 @@ def tile_wassvladlayer_pa_kernel(tc, x, mu, sigma, alpha, out):
     with (
         tc.tile_pool(name="const", bufs=1) as const,
         tc.tile_pool(name="load", bufs=LOADS_AHEAD + 2) as load,
-        tc.tile_pool(name="squares", bufs=SQUARE_LEAD + 2) as squares,
         tc.tile_pool(name="work", bufs=2) as work,
         tc.tile_pool(name="store", bufs=3) as store,
         tc.psum_pool(name="psum", bufs=2) as psum,
@@ -108,7 +121,7 @@ def tile_wassvladlayer_pa_kernel(tc, x, mu, sigma, alpha, out):
         def square_on_scalar(u):
             if not is_unit(u):
                 return
-            sq_grouped = squares.tile([P, UNIT, PACK], BF16, align_bytes=64)
+            sq_grouped = work.tile([P, UNIT, PACK], BF16, align_bytes=64)
             nc.scalar.activation(
                 out=sq_grouped[:, :cut, :].rearrange("p (c i) j -> p c j i", i=4),
                 in_=held["raw", u][:, :, :cut].rearrange("p j (c i) -> p c j i", i=4),
@@ -154,7 +167,7 @@ def tile_wassvladlayer_pa_kernel(tc, x, mu, sigma, alpha, out):
             nc.scalar.activation(
                 out=logits[:].rearrange("k g n -> k (g n)"), in_=held["acc", u][:], func=ACT.Identity, bias=bias[:, 0:1]
             )
-            logits_t = psum.tile([P, BLOCKS, P], F32, tag="by_point", bufs=3)
+            logits_t = psum.tile([P, BLOCKS, P], F32, tag="by_point")
             for g in range(BLOCKS):
                 nc.tensor.transpose(logits_t[:, g, :], logits[:, g, :], ident[:])
             held["logits_t", u] = logits_t
@@ -179,17 +192,24 @@ def tile_wassvladlayer_pa_kernel(tc, x, mu, sigma, alpha, out):
                     bias=held["neg_max", u][:, g : g + 1],
                     accum_out=total[:, g : g + 1],
                 )
-            held["expo", u] = (expo, total)
+            held["expo", u] = expo
+            held["total", u] = total
+
+        def invert_total(u):
+            if not is_unit(u):
+                return
+            inv_total = work.tile([P, BLOCKS], F32)
+            nc.vector.reciprocal(out=inv_total[:], in_=held["total", u][:])
+            held["inv_total", u] = inv_total
 
         def normalise_and_transpose(u):
             if not is_unit(u):
                 return
-            expo, total = held["expo", u]
-            inv_total = work.tile([P, BLOCKS], F32)
-            nc.vector.reciprocal(out=inv_total[:], in_=total[:])
             prob = work.tile([P, BLOCKS, P], F32)
             for g in range(BLOCKS):
-                nc.vector.tensor_scalar_mul(out=prob[:, g, :], in0=expo[:, g, :], scalar1=inv_total[:, g : g + 1])
+                nc.vector.tensor_scalar_mul(
+                    out=prob[:, g, :], in0=held["expo", u][:, g, :], scalar1=held["inv_total", u][:, g : g + 1]
+                )
             prob_t = psum.tile([P, BLOCKS, P], F32, tag="back")
             for g in range(BLOCKS):
                 nc.tensor.transpose(prob_t[:, g, :], prob[:, g, :], ident[:])
@@ -203,25 +223,28 @@ def tile_wassvladlayer_pa_kernel(tc, x, mu, sigma, alpha, out):
             nc.scalar.copy(out=result[:], in_=held["prob_t", u][:].rearrange("k g n -> k (g n)"))
             nc.sync.dma_start(out=out[b, :, cols], in_=result[:])
 
-        ident = const.tile([P, P], F32)
-        make_identity(nc, ident[:])
-        w_codes, w_scales, bias = prepare_clusters(nc, const, psum, mu, sigma, ident)
-        for u in range(LOADS_AHEAD):
-            load_x(u)
-        for u in range(SQUARE_LEAD):
-            square_on_scalar(u)
-        group_x(0)
-
-        for i in range(UNITS + LAST_STEP_LAG):
+        def run_round(i):
             load_x(i + LOADS_AHEAD)
             quantise("sq", i - 1)
             multiply(i - 1)
-            square_on_scalar(i + SQUARE_LEAD)
+            square_on_scalar(i)
             quantise("x", i)
+            invert_total(i - 3)
             square_on_vector(i)
             add_bias_and_transpose(i - 1)
             find_max(i - 2)
-            exponentiate(i - 3)
-            group_x(i + 1)
             store_out(i - LAST_STEP_LAG)
-            normalise_and_transpose(i - 4)
+            exponentiate(i - 2)
+            group_x(i + 1)
+            normalise_and_transpose(i - 3)
+
+        ident = const.tile([P, P], F32)
+        make_identity(nc, ident[:])
+        mu_raw, log_sc, s2, estimate = start_clusters(nc, const, mu, sigma)
+        for u in range(LOADS_AHEAD):
+            load_x(u)
+        group_x(0)
+        run_round(0)
+        w_codes, w_scales, bias = finish_clusters(nc, const, psum, ident, mu_raw, log_sc, s2, estimate)
+        for i in range(1, UNITS + LAST_STEP_LAG):
+            run_round(i)

@@ -20,7 +20,7 @@ UNITS_PER_BATCH = N // UNIT
 UNITS = B * UNITS_PER_BATCH
 LOADS_AHEAD = 3
 LAST_STEP_LAG = 4
-SCALAR_SQUARE_POINTS = 384
+SCALAR_SQUARE_POINTS = 368
 
 FLOPS = 2 * 2 * B * D * K * N
 
@@ -41,7 +41,7 @@ def start_clusters(nc, const, mu, sigma):
     return mu_raw, log_sc, s2, estimate
 
 
-def finish_clusters(nc, const, psum, ident, mu_raw, log_sc, s2, estimate):
+def combine_clusters(nc, const, psum, ident, mu_raw, log_sc, s2, estimate):
     inv_s2 = const.tile([P, PACK, K], F32)
     nc.vector.tensor_mul(out=inv_s2[:], in0=s2[:], in1=estimate[:])
     nc.vector.tensor_scalar(out=inv_s2[:], in0=inv_s2[:], scalar1=-1.0, scalar2=2.0, op0=ALU.mult, op1=ALU.add)
@@ -54,13 +54,6 @@ def finish_clusters(nc, const, psum, ident, mu_raw, log_sc, s2, estimate):
     w_grouped = const.tile([P, 2, K, PACK], BF16, align_bytes=64)
     nc.scalar.activation(out=w_grouped[:, 0], in_=inv_s2[:].rearrange("p j k -> p k j"), func=ACT.Copy, scale=-0.5)
     nc.scalar.copy(out=w_grouped[:, 1], in_=mu_inv[:].rearrange("p j k -> p k j"))
-    w_codes = const.tile([P, 2, K], U32, align_bytes=64)
-    w_scales = const.tile([P, 2, K], U8, align_bytes=64)
-    nc.vector.quantize_mx(
-        out=w_codes[:].rearrange("p w k -> p (w k)").bitcast(FP8X4),
-        scales=w_scales[:].rearrange("p w k -> p (w k)"),
-        in_=w_grouped[:].rearrange("p w k j -> p (w k j)"),
-    )
 
     sums = const.tile([P, 2], F32)
     unread = const.tile([P, 2, PACK * P], F32)
@@ -76,8 +69,19 @@ def finish_clusters(nc, const, psum, ident, mu_raw, log_sc, s2, estimate):
             accum_out=sums[:, t : t + 1],
         )
     bias = const.tile([P, 1], F32)
-    nc.vector.tensor_add(out=bias[:], in0=sums[:, 0:1], in1=sums[:, 1:2])
-    return w_codes, w_scales, bias
+    nc.scalar.activation(out=bias[:], in_=sums[:, 0:1], func=ACT.Identity, bias=sums[:, 1:2])
+    return w_grouped, bias
+
+
+def quantise_clusters(nc, const, w_grouped):
+    w_codes = const.tile([P, 2, K], U32, align_bytes=64)
+    w_scales = const.tile([P, 2, K], U8, align_bytes=64)
+    nc.vector.quantize_mx(
+        out=w_codes[:].rearrange("p w k -> p (w k)").bitcast(FP8X4),
+        scales=w_scales[:].rearrange("p w k -> p (w k)"),
+        in_=w_grouped[:].rearrange("p w k j -> p (w k j)"),
+    )
+    return w_codes, w_scales
 
 
 def tile_wassvladlayer_pa_kernel(tc, x, mu, sigma, alpha, out):
@@ -88,7 +92,6 @@ def tile_wassvladlayer_pa_kernel(tc, x, mu, sigma, alpha, out):
         tc.tile_pool(name="work", bufs=2) as work,
         tc.tile_pool(name="store", bufs=3) as store,
         tc.psum_pool(name="psum", bufs=2) as psum,
-        tc.manual_schedule(),
     ):
         held = {}
         cut = SCALAR_SQUARE_POINTS
@@ -223,14 +226,16 @@ def tile_wassvladlayer_pa_kernel(tc, x, mu, sigma, alpha, out):
             nc.scalar.copy(out=result[:], in_=held["prob_t", u][:].rearrange("k g n -> k (g n)"))
             nc.sync.dma_start(out=out[b, :, cols], in_=result[:])
 
-        def run_round(i):
+        def first_half(i):
             load_x(i + LOADS_AHEAD)
             quantise("sq", i - 1)
-            multiply(i - 1)
             square_on_scalar(i)
             quantise("x", i)
             invert_total(i - 3)
             square_on_vector(i)
+
+        def second_half(i):
+            multiply(i - 1)
             add_bias_and_transpose(i - 1)
             find_max(i - 2)
             store_out(i - LAST_STEP_LAG)
@@ -244,7 +249,12 @@ def tile_wassvladlayer_pa_kernel(tc, x, mu, sigma, alpha, out):
         for u in range(LOADS_AHEAD):
             load_x(u)
         group_x(0)
-        run_round(0)
-        w_codes, w_scales, bias = finish_clusters(nc, const, psum, ident, mu_raw, log_sc, s2, estimate)
-        for i in range(1, UNITS + LAST_STEP_LAG):
-            run_round(i)
+        first_half(0)
+        second_half(0)
+        w_grouped, bias = combine_clusters(nc, const, psum, ident, mu_raw, log_sc, s2, estimate)
+        first_half(1)
+        w_codes, w_scales = quantise_clusters(nc, const, w_grouped)
+        second_half(1)
+        for i in range(2, UNITS + LAST_STEP_LAG):
+            first_half(i)
+            second_half(i)

@@ -15,12 +15,12 @@ EPS = 1e-06
 P = 128
 PACK = 4
 UNIT = 512
-BLOCKS = UNIT // P
-UNITS_PER_BATCH = N // UNIT
-UNITS = B * UNITS_PER_BATCH
+CHUNKS = [256, 256, 512] + [1024] * (B * N // 1024 - 2) + [512, 256, 256]
+CHUNK_FIRSTS = [sum(CHUNKS[:c]) for c in range(len(CHUNKS))]
+UNITS = [(c, first, min(UNIT, width - first)) for c, width in enumerate(CHUNKS) for first in range(0, width, UNIT)]
 LOADS_AHEAD = 3
-LAST_STEP_LAG = 4
-SCALAR_SQUARE_POINTS = 368
+SCALAR_SHARE = 24
+SHARES = 32
 
 FLOPS = 2 * 2 * B * D * K * N
 
@@ -28,24 +28,31 @@ FLOPS = 2 * 2 * B * D * K * N
 def start_clusters(nc, const, mu, sigma):
     sig_raw = const.tile([P, PACK, K], BF16)
     mu_raw = const.tile([P, PACK, K], BF16)
-    nc.scalar.dma_start(out=sig_raw[:], in_=sigma.flatten_outer_dims().rearrange("(p j) k -> p j k", j=PACK))
-    nc.scalar.dma_start(out=mu_raw[:], in_=mu.flatten_outer_dims().rearrange("(p j) k -> p j k", j=PACK))
+    nc.sync.dma_start(out=sig_raw[:], in_=sigma.flatten_outer_dims().rearrange("(p j) k -> p j k", j=PACK))
+    nc.sync.dma_start(out=mu_raw[:], in_=mu.flatten_outer_dims().rearrange("(p j) k -> p j k", j=PACK))
     sc = const.tile([P, PACK, K], F32)
     nc.vector.tensor_scalar_max(out=sc[:], in0=sig_raw[:], scalar1=EPS)
     log_sc = const.tile([P, PACK, K], F32)
     nc.scalar.activation(out=log_sc[:], in_=sc[:], func=ACT.Ln)
     s2 = const.tile([P, PACK, K], F32)
-    nc.scalar.activation(out=s2[:], in_=sc[:], func=ACT.Square)
+    nc.vector.tensor_mul(out=s2[:], in0=sc[:], in1=sc[:])
     estimate = const.tile([P, PACK, K], F32)
     nc.scalar.activation(out=estimate[:], in_=log_sc[:], func=ACT.Exp, scale=-2.0)
     return mu_raw, log_sc, s2, estimate
 
 
-def combine_clusters(nc, const, psum, ident, mu_raw, log_sc, s2, estimate):
+def combine_clusters(nc, const, psum, mu_raw, log_sc, s2, estimate):
+    def flat(tile):
+        return tile[:].rearrange("p j k -> p (j k)")
+
+    minus_s2y = const.tile([P, PACK, K], F32)
+    nc.vector.scalar_tensor_tensor(
+        out=flat(minus_s2y), in0=flat(s2), scalar=-1.0, in1=flat(estimate), op0=ALU.mult, op1=ALU.mult
+    )
     inv_s2 = const.tile([P, PACK, K], F32)
-    nc.vector.tensor_mul(out=inv_s2[:], in0=s2[:], in1=estimate[:])
-    nc.vector.tensor_scalar(out=inv_s2[:], in0=inv_s2[:], scalar1=-1.0, scalar2=2.0, op0=ALU.mult, op1=ALU.add)
-    nc.vector.tensor_mul(out=inv_s2[:], in0=inv_s2[:], in1=estimate[:])
+    nc.vector.scalar_tensor_tensor(
+        out=flat(inv_s2), in0=flat(minus_s2y), scalar=2.0, in1=flat(estimate), op0=ALU.add, op1=ALU.mult
+    )
     mu_inv = const.tile([P, PACK, K], F32)
     nc.vector.tensor_mul(out=mu_inv[:], in0=mu_raw[:], in1=inv_s2[:])
     mu2_inv = const.tile([P, PACK, K], F32)
@@ -55,21 +62,21 @@ def combine_clusters(nc, const, psum, ident, mu_raw, log_sc, s2, estimate):
     nc.scalar.activation(out=w_grouped[:, 0], in_=inv_s2[:].rearrange("p j k -> p k j"), func=ACT.Copy, scale=-0.5)
     nc.scalar.copy(out=w_grouped[:, 1], in_=mu_inv[:].rearrange("p j k -> p k j"))
 
-    sums = const.tile([P, 2], F32)
-    unread = const.tile([P, 2, PACK * P], F32)
-    for t, (term, factor, tag) in enumerate(((mu2_inv, -0.5, "by_point"), (log_sc, -1.0, "back"))):
-        term_t = psum.tile([P, PACK, P], F32, tag=tag)
+    factors = const.tile([P, 2], F32)
+    nc.gpsimd.memset(factors[:, 0:1], -1.0)
+    nc.gpsimd.memset(factors[:, 1:2], -0.5)
+    bias_sum = psum.tile([P, 1], F32, tag="by_point")
+    for t, term in enumerate((log_sc, mu2_inv)):
         for j in range(PACK):
-            nc.tensor.transpose(term_t[:, j, :], term[:, j, :], ident[:])
-        nc.scalar.activation(
-            out=unread[:, t, :],
-            in_=term_t[:].rearrange("k j p -> k (j p)"),
-            func=ACT.Copy,
-            scale=factor,
-            accum_out=sums[:, t : t + 1],
-        )
+            nc.tensor.matmul(
+                out=bias_sum[:],
+                lhsT=term[:, j, :],
+                rhs=factors[:, t : t + 1],
+                start=(t == 0 and j == 0),
+                stop=(t == 1 and j == PACK - 1),
+            )
     bias = const.tile([P, 1], F32)
-    nc.scalar.activation(out=bias[:], in_=sums[:, 0:1], func=ACT.Identity, bias=sums[:, 1:2])
+    nc.scalar.copy(out=bias[:], in_=bias_sum[:])
     return w_grouped, bias
 
 
@@ -89,105 +96,121 @@ def tile_wassvladlayer_pa_kernel(tc, x, mu, sigma, alpha, out):
     with (
         tc.tile_pool(name="const", bufs=1) as const,
         tc.tile_pool(name="load", bufs=LOADS_AHEAD + 2) as load,
-        tc.tile_pool(name="work", bufs=2) as work,
+        tc.tile_pool(name="wide", bufs=2) as wide,
+        tc.tile_pool(name="soft", bufs=3) as soft,
         tc.tile_pool(name="store", bufs=3) as store,
-        tc.psum_pool(name="psum", bufs=2) as psum,
+        tc.psum_pool(name="psum_mx", bufs=2) as psum_mx,
+        tc.psum_pool(name="psum_t", bufs=3) as psum_t,
     ):
         held = {}
-        cut = SCALAR_SQUARE_POINTS
+
+        def is_chunk(c):
+            return 0 <= c < len(CHUNKS)
 
         def is_unit(u):
-            return 0 <= u < UNITS
+            return 0 <= u < len(UNITS)
 
-        def hbm_cols(u):
-            first = (u % UNITS_PER_BATCH) * UNIT
-            return u // UNITS_PER_BATCH, slice(first, first + UNIT)
+        def hbm_cols(first, width):
+            b, col = divmod(first, N)
+            return b, slice(col, col + width)
 
-        def load_x(u):
-            if not is_unit(u):
+        def scalar_points(c):
+            return CHUNKS[c] * SCALAR_SHARE // SHARES
+
+        def load_x(c):
+            if not is_chunk(c):
                 return
-            b, cols = hbm_cols(u)
-            raw = load.tile([P, PACK, UNIT], BF16)
+            b, cols = hbm_cols(CHUNK_FIRSTS[c], CHUNKS[c])
+            raw = load.tile([P, PACK, CHUNKS[c]], BF16)
             nc.sync.dma_start(out=raw[:], in_=x[b, :, cols].rearrange("(p j) n -> p j n", j=PACK))
-            held["raw", u] = raw
+            held["raw", c] = raw
 
-        def group_x(u):
-            if not is_unit(u):
+        def group_x(c):
+            if not is_chunk(c):
                 return
-            x_grouped = work.tile([P, UNIT, PACK], BF16, align_bytes=64)
+            x_grouped = wide.tile([P, CHUNKS[c], PACK], BF16, align_bytes=64)
             nc.vector.tensor_copy(
                 out=x_grouped[:].rearrange("p (c i) j -> p c j i", i=4),
-                in_=held["raw", u][:].rearrange("p j (c i) -> p c j i", i=4),
+                in_=held["raw", c][:].rearrange("p j (c i) -> p c j i", i=4),
             )
-            held["x", u] = x_grouped[:].rearrange("p n j -> p (n j)")
+            held["x", c] = x_grouped[:].rearrange("p n j -> p (n j)")
 
-        def square_on_scalar(u):
-            if not is_unit(u):
+        def square_on_scalar(c):
+            if not is_chunk(c):
                 return
-            sq_grouped = work.tile([P, UNIT, PACK], BF16, align_bytes=64)
-            nc.scalar.activation(
-                out=sq_grouped[:, :cut, :].rearrange("p (c i) j -> p c j i", i=4),
-                in_=held["raw", u][:, :, :cut].rearrange("p j (c i) -> p c j i", i=4),
-                func=ACT.Square,
-            )
-            held["sq", u] = sq_grouped[:].rearrange("p n j -> p (n j)")
+            sq_grouped = wide.tile([P, CHUNKS[c], PACK], BF16, align_bytes=64)
+            pieces = max(1, CHUNKS[c] // UNIT)
+            width = scalar_points(c) // pieces
+            for piece in range(pieces):
+                points = slice(piece * width, (piece + 1) * width)
+                nc.scalar.activation(
+                    out=sq_grouped[:, points, :].rearrange("p (c i) j -> p c j i", i=4),
+                    in_=held["raw", c][:, :, points].rearrange("p j (c i) -> p c j i", i=4),
+                    func=ACT.Square,
+                )
+            held["sq", c] = sq_grouped[:].rearrange("p n j -> p (n j)")
 
-        def square_on_vector(u):
-            if not is_unit(u):
+        def square_on_vector(c):
+            if not is_chunk(c):
                 return
-            rest = slice(cut * PACK, UNIT * PACK)
-            nc.vector.tensor_mul(out=held["sq", u][:, rest], in0=held["x", u][:, rest], in1=held["x", u][:, rest])
+            rest = slice(scalar_points(c) * PACK, CHUNKS[c] * PACK)
+            nc.vector.tensor_mul(out=held["sq", c][:, rest], in0=held["x", c][:, rest], in1=held["x", c][:, rest])
 
-        def quantise(what, u):
-            if not is_unit(u):
+        def quantise(what, c):
+            if not is_chunk(c):
                 return
-            codes = work.tile([P, UNIT], U32, align_bytes=64, tag=what + "_codes")
-            scales = work.tile([P, UNIT], U8, align_bytes=64, tag=what + "_scales")
-            nc.vector.quantize_mx(out=codes[:].bitcast(FP8X4), scales=scales[:], in_=held[what, u][:])
-            held[what + "_mx", u] = (codes, scales)
+            codes = wide.tile([P, CHUNKS[c]], U32, align_bytes=64, tag=what + "_codes")
+            scales = wide.tile([P, CHUNKS[c]], U8, align_bytes=64, tag=what + "_scales")
+            nc.vector.quantize_mx(out=codes[:].bitcast(FP8X4), scales=scales[:], in_=held[what, c][:])
+            held[what + "_mx", c] = (codes, scales)
 
         def multiply(u):
             if not is_unit(u):
                 return
-            acc = psum.tile([P, UNIT], F32, tag="by_cluster")
+            c, first, width = UNITS[u]
+            cols = slice(first, first + width)
+            acc = psum_mx.tile([P, width], F32)
             for w, what in enumerate(("sq_mx", "x_mx")):
-                codes, scales = held[what, u]
+                codes, scales = held[what, c]
                 nc.tensor.matmul_mx(
                     out=acc[:],
                     lhsT=w_codes[:, w, :].bitcast(FP8X4),
                     lhsT_scale=w_scales[:, w, :],
-                    rhs=codes[:].bitcast(FP8X4),
-                    rhs_scale=scales[:],
+                    rhs=codes[:, cols].bitcast(FP8X4),
+                    rhs_scale=scales[:, cols],
                     start=(w == 0),
                     stop=(w == 1),
                 )
             held["acc", u] = acc
 
+        def blocks_of(u):
+            return UNITS[u][2] // P
+
         def add_bias_and_transpose(u):
             if not is_unit(u):
                 return
-            logits = work.tile([P, BLOCKS, P], F32)
+            logits = soft.tile([P, blocks_of(u), P], F32)
             nc.scalar.activation(
                 out=logits[:].rearrange("k g n -> k (g n)"), in_=held["acc", u][:], func=ACT.Identity, bias=bias[:, 0:1]
             )
-            logits_t = psum.tile([P, BLOCKS, P], F32, tag="by_point")
-            for g in range(BLOCKS):
+            logits_t = psum_t.tile([P, blocks_of(u), P], F32, tag="by_point")
+            for g in range(blocks_of(u)):
                 nc.tensor.transpose(logits_t[:, g, :], logits[:, g, :], ident[:])
             held["logits_t", u] = logits_t
 
         def find_max(u):
             if not is_unit(u):
                 return
-            neg_max = work.tile([P, BLOCKS], F32)
+            neg_max = soft.tile([P, blocks_of(u)], F32)
             nc.vector.tensor_reduce(out=neg_max[:], in_=held["logits_t", u][:], axis=AXIS.X, op=ALU.max, negate=True)
             held["neg_max", u] = neg_max
 
         def exponentiate(u):
             if not is_unit(u):
                 return
-            expo = work.tile([P, BLOCKS, P], F32)
-            total = work.tile([P, BLOCKS], F32)
-            for g in range(BLOCKS):
+            expo = soft.tile([P, blocks_of(u), P], F32)
+            total = soft.tile([P, blocks_of(u)], F32)
+            for g in range(blocks_of(u)):
                 nc.scalar.activation(
                     out=expo[:, g, :],
                     in_=held["logits_t", u][:, g, :],
@@ -201,60 +224,70 @@ def tile_wassvladlayer_pa_kernel(tc, x, mu, sigma, alpha, out):
         def invert_total(u):
             if not is_unit(u):
                 return
-            inv_total = work.tile([P, BLOCKS], F32)
+            inv_total = soft.tile([P, blocks_of(u)], F32)
             nc.vector.reciprocal(out=inv_total[:], in_=held["total", u][:])
             held["inv_total", u] = inv_total
 
         def normalise_and_transpose(u):
             if not is_unit(u):
                 return
-            prob = work.tile([P, BLOCKS, P], F32)
-            for g in range(BLOCKS):
+            prob = soft.tile([P, blocks_of(u), P], F32)
+            for g in range(blocks_of(u)):
                 nc.vector.tensor_scalar_mul(
                     out=prob[:, g, :], in0=held["expo", u][:, g, :], scalar1=held["inv_total", u][:, g : g + 1]
                 )
-            prob_t = psum.tile([P, BLOCKS, P], F32, tag="back")
-            for g in range(BLOCKS):
+            prob_t = psum_t.tile([P, blocks_of(u), P], F32, tag="back")
+            for g in range(blocks_of(u)):
                 nc.tensor.transpose(prob_t[:, g, :], prob[:, g, :], ident[:])
             held["prob_t", u] = prob_t
 
         def store_out(u):
             if not is_unit(u):
                 return
-            b, cols = hbm_cols(u)
-            result = store.tile([P, UNIT], F32)
+            c, first, width = UNITS[u]
+            b, cols = hbm_cols(CHUNK_FIRSTS[c] + first, width)
+            result = store.tile([P, width], F32)
             nc.scalar.copy(out=result[:], in_=held["prob_t", u][:].rearrange("k g n -> k (g n)"))
             nc.sync.dma_start(out=out[b, :, cols], in_=result[:])
 
-        def first_half(i):
-            load_x(i + LOADS_AHEAD)
-            quantise("sq", i - 1)
-            square_on_scalar(i)
-            quantise("x", i)
-            invert_total(i - 3)
-            square_on_vector(i)
+        def front_steps(r):
+            load_x(r + LOADS_AHEAD)
+            quantise("sq", r - 1)
+            square_on_scalar(r)
+            quantise("x", r)
 
-        def second_half(i):
-            multiply(i - 1)
-            add_bias_and_transpose(i - 1)
-            find_max(i - 2)
-            store_out(i - LAST_STEP_LAG)
-            exponentiate(i - 2)
-            group_x(i + 1)
-            normalise_and_transpose(i - 3)
+        def middle_steps(r):
+            square_on_vector(r)
+            group_x(r + 1)
+
+        def back_steps(u):
+            multiply(u)
+            add_bias_and_transpose(u)
+            invert_total(u - 2)
+            find_max(u - 1)
+            store_out(u - 3)
+            exponentiate(u - 1)
+            normalise_and_transpose(u - 2)
 
         ident = const.tile([P, P], F32)
         make_identity(nc, ident[:])
         mu_raw, log_sc, s2, estimate = start_clusters(nc, const, mu, sigma)
-        for u in range(LOADS_AHEAD):
-            load_x(u)
+        for c in range(LOADS_AHEAD):
+            load_x(c)
         group_x(0)
-        first_half(0)
-        second_half(0)
-        w_grouped, bias = combine_clusters(nc, const, psum, ident, mu_raw, log_sc, s2, estimate)
-        first_half(1)
-        w_codes, w_scales = quantise_clusters(nc, const, w_grouped)
-        second_half(1)
-        for i in range(2, UNITS + LAST_STEP_LAG):
-            first_half(i)
-            second_half(i)
+        front_steps(0)
+        middle_steps(0)
+        w_grouped, bias = combine_clusters(nc, const, psum_t, mu_raw, log_sc, s2, estimate)
+        for r in range(1, len(CHUNKS) + 1):
+            front_steps(r)
+            if r == 1:
+                w_codes, w_scales = quantise_clusters(nc, const, w_grouped)
+            units = [u for u in range(len(UNITS)) if UNITS[u][0] == r - 1]
+            half = (len(units) + 1) // 2
+            for u in units[:half]:
+                back_steps(u)
+            middle_steps(r)
+            for u in units[half:]:
+                back_steps(u)
+        for u in range(len(UNITS), len(UNITS) + 3):
+            back_steps(u)

@@ -19,7 +19,7 @@ CHUNKS = [256, 256, 512] + [1024] * (B * N // 1024 - 2) + [512, 256, 256]
 CHUNK_FIRSTS = [sum(CHUNKS[:c]) for c in range(len(CHUNKS))]
 UNITS = [(c, first, min(UNIT, width - first)) for c, width in enumerate(CHUNKS) for first in range(0, width, UNIT)]
 LOADS_AHEAD = 3
-SCALAR_SHARE = 24
+SCALAR_SHARE = 23
 SHARES = 32
 
 FLOPS = 2 * 2 * B * D * K * N
@@ -32,35 +32,25 @@ def start_clusters(nc, const, mu, sigma):
     nc.sync.dma_start(out=mu_raw[:], in_=mu.flatten_outer_dims().rearrange("(p j) k -> p j k", j=PACK))
     sc = const.tile([P, PACK, K], F32)
     nc.vector.tensor_scalar_max(out=sc[:], in0=sig_raw[:], scalar1=EPS)
+    mu2 = const.tile([P, PACK, K], F32)
+    nc.vector.tensor_mul(out=mu2[:], in0=mu_raw[:], in1=mu_raw[:])
     log_sc = const.tile([P, PACK, K], F32)
     nc.scalar.activation(out=log_sc[:], in_=sc[:], func=ACT.Ln)
-    s2 = const.tile([P, PACK, K], F32)
-    nc.vector.tensor_mul(out=s2[:], in0=sc[:], in1=sc[:])
-    estimate = const.tile([P, PACK, K], F32)
-    nc.scalar.activation(out=estimate[:], in_=log_sc[:], func=ACT.Exp, scale=-2.0)
-    return mu_raw, log_sc, s2, estimate
-
-
-def combine_clusters(nc, const, psum, mu_raw, log_sc, s2, estimate):
-    def flat(tile):
-        return tile[:].rearrange("p j k -> p (j k)")
-
-    minus_s2y = const.tile([P, PACK, K], F32)
-    nc.vector.scalar_tensor_tensor(
-        out=flat(minus_s2y), in0=flat(s2), scalar=-1.0, in1=flat(estimate), op0=ALU.mult, op1=ALU.mult
-    )
     inv_s2 = const.tile([P, PACK, K], F32)
-    nc.vector.scalar_tensor_tensor(
-        out=flat(inv_s2), in0=flat(minus_s2y), scalar=2.0, in1=flat(estimate), op0=ALU.add, op1=ALU.mult
-    )
-    mu_inv = const.tile([P, PACK, K], F32)
-    nc.vector.tensor_mul(out=mu_inv[:], in0=mu_raw[:], in1=inv_s2[:])
-    mu2_inv = const.tile([P, PACK, K], F32)
-    nc.vector.tensor_mul(out=mu2_inv[:], in0=mu_raw[:], in1=mu_inv[:])
+    nc.scalar.activation(out=inv_s2[:], in_=log_sc[:], func=ACT.Exp, scale=-2.0)
+    return mu_raw, mu2, log_sc, inv_s2
 
+
+def combine_clusters(nc, const, psum, mu_raw, mu2, log_sc, inv_s2):
     w_grouped = const.tile([P, 2, K, PACK], BF16, align_bytes=64)
-    nc.scalar.activation(out=w_grouped[:, 0], in_=inv_s2[:].rearrange("p j k -> p k j"), func=ACT.Copy, scale=-0.5)
-    nc.scalar.copy(out=w_grouped[:, 1], in_=mu_inv[:].rearrange("p j k -> p k j"))
+
+    def grouped(tile):
+        return tile[:].rearrange("p j k -> p k j")
+
+    nc.scalar.activation(out=w_grouped[:, 0], in_=grouped(inv_s2), func=ACT.Copy, scale=-0.5)
+    nc.vector.tensor_mul(out=w_grouped[:, 1], in0=grouped(mu_raw), in1=grouped(inv_s2))
+    mu2_inv = const.tile([P, PACK, K], F32)
+    nc.vector.tensor_mul(out=mu2_inv[:], in0=mu2[:], in1=inv_s2[:])
 
     factors = const.tile([P, 2], F32)
     nc.gpsimd.memset(factors[:, 0:1], -1.0)
@@ -271,13 +261,13 @@ def tile_wassvladlayer_pa_kernel(tc, x, mu, sigma, alpha, out):
 
         ident = const.tile([P, P], F32)
         make_identity(nc, ident[:])
-        mu_raw, log_sc, s2, estimate = start_clusters(nc, const, mu, sigma)
+        mu_raw, mu2, log_sc, inv_s2 = start_clusters(nc, const, mu, sigma)
         for c in range(LOADS_AHEAD):
             load_x(c)
         group_x(0)
         front_steps(0)
         middle_steps(0)
-        w_grouped, bias = combine_clusters(nc, const, psum_t, mu_raw, log_sc, s2, estimate)
+        w_grouped, bias = combine_clusters(nc, const, psum_t, mu_raw, mu2, log_sc, inv_s2)
         for r in range(1, len(CHUNKS) + 1):
             front_steps(r)
             if r == 1:

@@ -19,7 +19,9 @@ CHUNKS = [256, 256, 512] + [1024] * (B * N // 1024 - 2) + [512, 256, 256]
 CHUNK_FIRSTS = [sum(CHUNKS[:c]) for c in range(len(CHUNKS))]
 UNITS = [(c, first, min(UNIT, width - first)) for c, width in enumerate(CHUNKS) for first in range(0, width, UNIT)]
 LOADS_AHEAD = 3
-SCALAR_SHARE = 23
+VECTOR_ONLY_FIRST = 2
+VECTOR_ONLY_LAST = 2
+SCALAR_SHARE = 24
 SHARES = 32
 
 FLOPS = 2 * 2 * B * D * K * N
@@ -87,7 +89,7 @@ def tile_wassvladlayer_pa_kernel(tc, x, mu, sigma, alpha, out):
         tc.tile_pool(name="const", bufs=1) as const,
         tc.tile_pool(name="load", bufs=LOADS_AHEAD + 2) as load,
         tc.tile_pool(name="wide", bufs=2) as wide,
-        tc.tile_pool(name="soft", bufs=3) as soft,
+        tc.tile_pool(name="soft", bufs=5) as soft,
         tc.tile_pool(name="store", bufs=3) as store,
         tc.psum_pool(name="psum_mx", bufs=2) as psum_mx,
         tc.psum_pool(name="psum_t", bufs=3) as psum_t,
@@ -105,7 +107,8 @@ def tile_wassvladlayer_pa_kernel(tc, x, mu, sigma, alpha, out):
             return b, slice(col, col + width)
 
         def scalar_points(c):
-            return CHUNKS[c] * SCALAR_SHARE // SHARES
+            alone = c < VECTOR_ONLY_FIRST or c >= len(CHUNKS) - VECTOR_ONLY_LAST
+            return 0 if alone else CHUNKS[c] * SCALAR_SHARE // SHARES
 
         def load_x(c):
             if not is_chunk(c):
@@ -115,43 +118,43 @@ def tile_wassvladlayer_pa_kernel(tc, x, mu, sigma, alpha, out):
             nc.sync.dma_start(out=raw[:], in_=x[b, :, cols].rearrange("(p j) n -> p j n", j=PACK))
             held["raw", c] = raw
 
-        def group_x(c):
+        def group_on_scalar(c):
             if not is_chunk(c):
                 return
             x_grouped = wide.tile([P, CHUNKS[c], PACK], BF16, align_bytes=64)
-            nc.vector.tensor_copy(
-                out=x_grouped[:].rearrange("p (c i) j -> p c j i", i=4),
-                in_=held["raw", c][:].rearrange("p j (c i) -> p c j i", i=4),
-            )
-            held["x", c] = x_grouped[:].rearrange("p n j -> p (n j)")
-
-        def square_on_scalar(c):
-            if not is_chunk(c):
-                return
-            sq_grouped = wide.tile([P, CHUNKS[c], PACK], BF16, align_bytes=64)
-            pieces = max(1, CHUNKS[c] // UNIT)
-            width = scalar_points(c) // pieces
+            pieces = max(1, CHUNKS[c] // UNIT) if scalar_points(c) else 0
+            width = scalar_points(c) // max(1, pieces)
             for piece in range(pieces):
                 points = slice(piece * width, (piece + 1) * width)
-                nc.scalar.activation(
-                    out=sq_grouped[:, points, :].rearrange("p (c i) j -> p c j i", i=4),
+                nc.scalar.copy(
+                    out=x_grouped[:, points, :].rearrange("p (c i) j -> p c j i", i=4),
                     in_=held["raw", c][:, :, points].rearrange("p j (c i) -> p c j i", i=4),
-                    func=ACT.Square,
                 )
-            held["sq", c] = sq_grouped[:].rearrange("p n j -> p (n j)")
+            held["x_tile", c] = x_grouped
+            held["x", c] = x_grouped[:].rearrange("p n j -> p (n j)")
 
-        def square_on_vector(c):
+        def group_on_vector(c):
             if not is_chunk(c):
                 return
-            rest = slice(scalar_points(c) * PACK, CHUNKS[c] * PACK)
-            nc.vector.tensor_mul(out=held["sq", c][:, rest], in0=held["x", c][:, rest], in1=held["x", c][:, rest])
+            rest = slice(scalar_points(c), CHUNKS[c])
+            nc.vector.tensor_copy(
+                out=held["x_tile", c][:, rest, :].rearrange("p (c i) j -> p c j i", i=4),
+                in_=held["raw", c][:, :, rest].rearrange("p j (c i) -> p c j i", i=4),
+            )
+
+        def square(c):
+            if not is_chunk(c):
+                return
+            sq_grouped = wide.tile([P, CHUNKS[c] * PACK], BF16, align_bytes=64)
+            nc.vector.tensor_mul(out=sq_grouped[:], in0=held["x", c], in1=held["x", c])
+            held["sq", c] = sq_grouped[:]
 
         def quantise(what, c):
             if not is_chunk(c):
                 return
             codes = wide.tile([P, CHUNKS[c]], U32, align_bytes=64, tag=what + "_codes")
             scales = wide.tile([P, CHUNKS[c]], U8, align_bytes=64, tag=what + "_scales")
-            nc.vector.quantize_mx(out=codes[:].bitcast(FP8X4), scales=scales[:], in_=held[what, c][:])
+            nc.vector.quantize_mx(out=codes[:].bitcast(FP8X4), scales=scales[:], in_=held[what, c])
             held[what + "_mx", c] = (codes, scales)
 
         def multiply(u):
@@ -243,28 +246,29 @@ def tile_wassvladlayer_pa_kernel(tc, x, mu, sigma, alpha, out):
         def front_steps(r):
             load_x(r + LOADS_AHEAD)
             quantise("sq", r - 1)
-            square_on_scalar(r)
+            group_on_scalar(r + 1)
             quantise("x", r)
 
         def middle_steps(r):
-            square_on_vector(r)
-            group_x(r + 1)
+            square(r)
+            group_on_vector(r + 1)
 
         def back_steps(u):
             multiply(u)
             add_bias_and_transpose(u)
-            invert_total(u - 2)
-            find_max(u - 1)
-            store_out(u - 3)
-            exponentiate(u - 1)
-            normalise_and_transpose(u - 2)
+            invert_total(u - 4)
+            find_max(u - 2)
+            store_out(u - 5)
+            exponentiate(u - 2)
+            normalise_and_transpose(u - 4)
 
         ident = const.tile([P, P], F32)
         make_identity(nc, ident[:])
         mu_raw, mu2, log_sc, inv_s2 = start_clusters(nc, const, mu, sigma)
         for c in range(LOADS_AHEAD):
             load_x(c)
-        group_x(0)
+        group_on_scalar(0)
+        group_on_vector(0)
         front_steps(0)
         middle_steps(0)
         w_grouped, bias = combine_clusters(nc, const, psum_t, mu_raw, mu2, log_sc, inv_s2)
@@ -279,5 +283,5 @@ def tile_wassvladlayer_pa_kernel(tc, x, mu, sigma, alpha, out):
             middle_steps(r)
             for u in units[half:]:
                 back_steps(u)
-        for u in range(len(UNITS), len(UNITS) + 3):
+        for u in range(len(UNITS), len(UNITS) + 5):
             back_steps(u)

@@ -21,7 +21,7 @@ UNITS = [(c, first, min(UNIT, width - first)) for c, width in enumerate(CHUNKS) 
 LOADS_AHEAD = 3
 VECTOR_ONLY_FIRST = 2
 VECTOR_ONLY_LAST = 2
-SCALAR_SHARE = 24
+SCALAR_SHARE = 26
 SHARES = 32
 
 FLOPS = 2 * 2 * B * D * K * N

@@ -21,8 +21,10 @@ UNITS = [(c, first, min(UNIT, width - first)) for c, width in enumerate(CHUNKS) 
 LOADS_AHEAD = 3
 VECTOR_ONLY_FIRST = 2
 VECTOR_ONLY_LAST = 2
-SCALAR_SHARE = 26
+SCALAR_SHARE = 20
+TENSOR_SHARE = 6
 SHARES = 32
+TENSOR_POINTS = 96
 
 FLOPS = 2 * 2 * B * D * K * N
 
@@ -93,6 +95,8 @@ def tile_wassvladlayer_pa_kernel(tc, x, mu, sigma, alpha, out):
         tc.tile_pool(name="store", bufs=3) as store,
         tc.psum_pool(name="psum_mx", bufs=2) as psum_mx,
         tc.psum_pool(name="psum_t", bufs=3) as psum_t,
+        tc.psum_pool(name="psum_b", bufs=2) as psum_b,
+        tc.psum_pool(name="psum_g", bufs=1) as psum_g,
     ):
         held = {}
 
@@ -106,9 +110,10 @@ def tile_wassvladlayer_pa_kernel(tc, x, mu, sigma, alpha, out):
             b, col = divmod(first, N)
             return b, slice(col, col + width)
 
-        def scalar_points(c):
-            alone = c < VECTOR_ONLY_FIRST or c >= len(CHUNKS) - VECTOR_ONLY_LAST
-            return 0 if alone else CHUNKS[c] * SCALAR_SHARE // SHARES
+        def grouping_cuts(c):
+            if c < VECTOR_ONLY_FIRST or c >= len(CHUNKS) - VECTOR_ONLY_LAST:
+                return 0, 0
+            return CHUNKS[c] * SCALAR_SHARE // SHARES, CHUNKS[c] * (SCALAR_SHARE + TENSOR_SHARE) // SHARES
 
         def load_x(c):
             if not is_chunk(c):
@@ -122,10 +127,10 @@ def tile_wassvladlayer_pa_kernel(tc, x, mu, sigma, alpha, out):
             if not is_chunk(c):
                 return
             x_grouped = wide.tile([P, CHUNKS[c], PACK], BF16, align_bytes=64)
-            pieces = max(1, CHUNKS[c] // UNIT) if scalar_points(c) else 0
-            width = scalar_points(c) // max(1, pieces)
+            cut = grouping_cuts(c)[0]
+            pieces = max(1, CHUNKS[c] // UNIT) if cut else 0
             for piece in range(pieces):
-                points = slice(piece * width, (piece + 1) * width)
+                points = slice(piece * cut // pieces, (piece + 1) * cut // pieces)
                 nc.scalar.copy(
                     out=x_grouped[:, points, :].rearrange("p (c i) j -> p c j i", i=4),
                     in_=held["raw", c][:, :, points].rearrange("p j (c i) -> p c j i", i=4),
@@ -133,10 +138,30 @@ def tile_wassvladlayer_pa_kernel(tc, x, mu, sigma, alpha, out):
             held["x_tile", c] = x_grouped
             held["x", c] = x_grouped[:].rearrange("p n j -> p (n j)")
 
+        def group_on_tensor(c):
+            if not is_chunk(c):
+                return
+            first, end = grouping_cuts(c)
+            if first == end:
+                return
+            bank = psum_g.tile([P, end - first, PACK], BF16)
+            for start in range(first, end, TENSOR_POINTS):
+                points = slice(start, min(start + TENSOR_POINTS, end))
+                nc.tensor.matmul(
+                    out=bank[:, points.start - first : points.stop - first, :],
+                    lhsT=ident_bf16[:],
+                    rhs=held["raw", c][:, :, points].rearrange("p j n -> p n j"),
+                    start=True,
+                    stop=True,
+                )
+            nc.scalar.copy(
+                out=held["x", c][:, first * PACK : end * PACK], in_=bank[:].rearrange("p n j -> p (n j)")
+            )
+
         def group_on_vector(c):
             if not is_chunk(c):
                 return
-            rest = slice(scalar_points(c), CHUNKS[c])
+            rest = slice(grouping_cuts(c)[1], CHUNKS[c])
             nc.vector.tensor_copy(
                 out=held["x_tile", c][:, rest, :].rearrange("p (c i) j -> p c j i", i=4),
                 in_=held["raw", c][:, :, rest].rearrange("p j (c i) -> p c j i", i=4),
@@ -229,7 +254,7 @@ def tile_wassvladlayer_pa_kernel(tc, x, mu, sigma, alpha, out):
                 nc.vector.tensor_scalar_mul(
                     out=prob[:, g, :], in0=held["expo", u][:, g, :], scalar1=held["inv_total", u][:, g : g + 1]
                 )
-            prob_t = psum_t.tile([P, blocks_of(u), P], F32, tag="back")
+            prob_t = psum_b.tile([P, blocks_of(u), P], F32)
             for g in range(blocks_of(u)):
                 nc.tensor.transpose(prob_t[:, g, :], prob[:, g, :], ident[:])
             held["prob_t", u] = prob_t
@@ -247,6 +272,7 @@ def tile_wassvladlayer_pa_kernel(tc, x, mu, sigma, alpha, out):
             load_x(r + LOADS_AHEAD)
             quantise("sq", r - 1)
             group_on_scalar(r + 1)
+            group_on_tensor(r + 1)
             quantise("x", r)
 
         def middle_steps(r):
@@ -264,10 +290,13 @@ def tile_wassvladlayer_pa_kernel(tc, x, mu, sigma, alpha, out):
 
         ident = const.tile([P, P], F32)
         make_identity(nc, ident[:])
+        ident_bf16 = const.tile([P, P], BF16)
+        make_identity(nc, ident_bf16[:])
         mu_raw, mu2, log_sc, inv_s2 = start_clusters(nc, const, mu, sigma)
         for c in range(LOADS_AHEAD):
             load_x(c)
         group_on_scalar(0)
+        group_on_tensor(0)
         group_on_vector(0)
         front_steps(0)
         middle_steps(0)

@@ -21,10 +21,11 @@ UNITS = [(c, first, min(UNIT, width - first)) for c, width in enumerate(CHUNKS) 
 LOADS_AHEAD = 3
 VECTOR_ONLY_FIRST = 2
 VECTOR_ONLY_LAST = 2
-SCALAR_SHARE = 20
-TENSOR_SHARE = 6
+SCALAR_SHARE = 22
+TENSOR_SHARE = 4
+TENSOR_FIRST = 5
 SHARES = 32
-TENSOR_POINTS = 96
+TENSOR_POINTS = 128
 
 FLOPS = 2 * 2 * B * D * K * N
 
@@ -92,7 +93,7 @@ def tile_wassvladlayer_pa_kernel(tc, x, mu, sigma, alpha, out):
         tc.tile_pool(name="load", bufs=LOADS_AHEAD + 2) as load,
         tc.tile_pool(name="wide", bufs=2) as wide,
         tc.tile_pool(name="soft", bufs=5) as soft,
-        tc.tile_pool(name="store", bufs=3) as store,
+        tc.tile_pool(name="store", bufs=6) as store,
         tc.psum_pool(name="psum_mx", bufs=2) as psum_mx,
         tc.psum_pool(name="psum_t", bufs=3) as psum_t,
         tc.psum_pool(name="psum_b", bufs=2) as psum_b,
@@ -113,7 +114,8 @@ def tile_wassvladlayer_pa_kernel(tc, x, mu, sigma, alpha, out):
         def grouping_cuts(c):
             if c < VECTOR_ONLY_FIRST or c >= len(CHUNKS) - VECTOR_ONLY_LAST:
                 return 0, 0
-            return CHUNKS[c] * SCALAR_SHARE // SHARES, CHUNKS[c] * (SCALAR_SHARE + TENSOR_SHARE) // SHARES
+            share = SCALAR_SHARE if c >= TENSOR_FIRST else SCALAR_SHARE + TENSOR_SHARE
+            return CHUNKS[c] * share // SHARES, CHUNKS[c] * (SCALAR_SHARE + TENSOR_SHARE) // SHARES
 
         def load_x(c):
             if not is_chunk(c):

import concourse.mybir as mybir
from concourse.masks import make_identity

F32 = mybir.dt.float32
BF16 = mybir.dt.bfloat16
U32 = mybir.dt.uint32
U8 = mybir.dt.uint8
FP8X4 = mybir.dt.float8_e4m3fn_x4
ALU = mybir.AluOpType
ACT = mybir.ActivationFunctionType
AXIS = mybir.AxisListType

B, D, N, K = 4, 512, 4096, 128
EPS = 1e-06
P = 128
PACK = 4
UNIT = 512
CHUNKS = [256, 256, 512] + [1024] * (B * N // 1024 - 2) + [512, 256, 256]
CHUNK_FIRSTS = [sum(CHUNKS[:c]) for c in range(len(CHUNKS))]
UNITS = [(c, first, min(UNIT, width - first)) for c, width in enumerate(CHUNKS) for first in range(0, width, UNIT)]
LOADS_AHEAD = 3
VECTOR_ONLY_FIRST = 2
VECTOR_ONLY_LAST = 2
SCALAR_SHARE = 22
TENSOR_SHARE = 4
TENSOR_FIRST = 5
SHARES = 32
TENSOR_POINTS = 128

FLOPS = 2 * 2 * B * D * K * N


def start_clusters(nc, const, mu, sigma):
    sig_raw = const.tile([P, PACK, K], BF16)
    mu_raw = const.tile([P, PACK, K], BF16)
    nc.sync.dma_start(out=sig_raw[:], in_=sigma.flatten_outer_dims().rearrange("(p j) k -> p j k", j=PACK))
    nc.sync.dma_start(out=mu_raw[:], in_=mu.flatten_outer_dims().rearrange("(p j) k -> p j k", j=PACK))
    sc = const.tile([P, PACK, K], F32)
    nc.vector.tensor_scalar_max(out=sc[:], in0=sig_raw[:], scalar1=EPS)
    mu2 = const.tile([P, PACK, K], F32)
    nc.vector.tensor_mul(out=mu2[:], in0=mu_raw[:], in1=mu_raw[:])
    log_sc = const.tile([P, PACK, K], F32)
    nc.scalar.activation(out=log_sc[:], in_=sc[:], func=ACT.Ln)
    inv_s2 = const.tile([P, PACK, K], F32)
    nc.scalar.activation(out=inv_s2[:], in_=log_sc[:], func=ACT.Exp, scale=-2.0)
    return mu_raw, mu2, log_sc, inv_s2


def combine_clusters(nc, const, psum, mu_raw, mu2, log_sc, inv_s2):
    w_grouped = const.tile([P, 2, K, PACK], BF16, align_bytes=64)

    def grouped(tile):
        return tile[:].rearrange("p j k -> p k j")

    nc.scalar.activation(out=w_grouped[:, 0], in_=grouped(inv_s2), func=ACT.Copy, scale=-0.5)
    nc.vector.tensor_mul(out=w_grouped[:, 1], in0=grouped(mu_raw), in1=grouped(inv_s2))
    mu2_inv = const.tile([P, PACK, K], F32)
    nc.vector.tensor_mul(out=mu2_inv[:], in0=mu2[:], in1=inv_s2[:])

    factors = const.tile([P, 2], F32)
    nc.gpsimd.memset(factors[:, 0:1], -1.0)
    nc.gpsimd.memset(factors[:, 1:2], -0.5)
    bias_sum = psum.tile([P, 1], F32, tag="by_point")
    for t, term in enumerate((log_sc, mu2_inv)):
        for j in range(PACK):
            nc.tensor.matmul(
                out=bias_sum[:],
                lhsT=term[:, j, :],
                rhs=factors[:, t : t + 1],
                start=(t == 0 and j == 0),
                stop=(t == 1 and j == PACK - 1),
            )
    bias = const.tile([P, 1], F32)
    nc.scalar.copy(out=bias[:], in_=bias_sum[:])
    return w_grouped, bias


def quantise_clusters(nc, const, w_grouped):
    w_codes = const.tile([P, 2, K], U32, align_bytes=64)
    w_scales = const.tile([P, 2, K], U8, align_bytes=64)
    nc.vector.quantize_mx(
        out=w_codes[:].rearrange("p w k -> p (w k)").bitcast(FP8X4),
        scales=w_scales[:].rearrange("p w k -> p (w k)"),
        in_=w_grouped[:].rearrange("p w k j -> p (w k j)"),
    )
    return w_codes, w_scales


def tile_wassvladlayer_pa_kernel(tc, x, mu, sigma, alpha, out):
    nc = tc.nc
    with (
        tc.tile_pool(name="const", bufs=1) as const,
        tc.tile_pool(name="load", bufs=LOADS_AHEAD + 2) as load,
        tc.tile_pool(name="wide", bufs=2) as wide,
        tc.tile_pool(name="soft", bufs=5) as soft,
        tc.tile_pool(name="store", bufs=6) as store,
        tc.psum_pool(name="psum_mx", bufs=2) as psum_mx,
        tc.psum_pool(name="psum_t", bufs=3) as psum_t,
        tc.psum_pool(name="psum_b", bufs=2) as psum_b,
        tc.psum_pool(name="psum_g", bufs=1) as psum_g,
    ):
        held = {}

        def is_chunk(c):
            return 0 <= c < len(CHUNKS)

        def is_unit(u):
            return 0 <= u < len(UNITS)

        def hbm_cols(first, width):
            b, col = divmod(first, N)
            return b, slice(col, col + width)

        def grouping_cuts(c):
            if c < VECTOR_ONLY_FIRST or c >= len(CHUNKS) - VECTOR_ONLY_LAST:
                return 0, 0
            share = SCALAR_SHARE if c >= TENSOR_FIRST else SCALAR_SHARE + TENSOR_SHARE
            return CHUNKS[c] * share // SHARES, CHUNKS[c] * (SCALAR_SHARE + TENSOR_SHARE) // SHARES

        def load_x(c):
            if not is_chunk(c):
                return
            b, cols = hbm_cols(CHUNK_FIRSTS[c], CHUNKS[c])
            raw = load.tile([P, PACK, CHUNKS[c]], BF16)
            nc.sync.dma_start(out=raw[:], in_=x[b, :, cols].rearrange("(p j) n -> p j n", j=PACK))
            held["raw", c] = raw

        def group_on_scalar(c):
            if not is_chunk(c):
                return
            x_grouped = wide.tile([P, CHUNKS[c], PACK], BF16, align_bytes=64)
            cut = grouping_cuts(c)[0]
            pieces = max(1, CHUNKS[c] // UNIT) if cut else 0
            for piece in range(pieces):
                points = slice(piece * cut // pieces, (piece + 1) * cut // pieces)
                nc.scalar.copy(
                    out=x_grouped[:, points, :].rearrange("p (c i) j -> p c j i", i=4),
                    in_=held["raw", c][:, :, points].rearrange("p j (c i) -> p c j i", i=4),
                )
            held["x_tile", c] = x_grouped
            held["x", c] = x_grouped[:].rearrange("p n j -> p (n j)")

        def group_on_tensor(c):
            if not is_chunk(c):
                return
            first, end = grouping_cuts(c)
            if first == end:
                return
            bank = psum_g.tile([P, end - first, PACK], BF16)
            for start in range(first, end, TENSOR_POINTS):
                points = slice(start, min(start + TENSOR_POINTS, end))
                nc.tensor.matmul(
                    out=bank[:, points.start - first : points.stop - first, :],
                    lhsT=ident_bf16[:],
                    rhs=held["raw", c][:, :, points].rearrange("p j n -> p n j"),
                    start=True,
                    stop=True,
                )
            nc.scalar.copy(
                out=held["x", c][:, first * PACK : end * PACK], in_=bank[:].rearrange("p n j -> p (n j)")
            )

        def group_on_vector(c):
            if not is_chunk(c):
                return
            rest = slice(grouping_cuts(c)[1], CHUNKS[c])
            nc.vector.tensor_copy(
                out=held["x_tile", c][:, rest, :].rearrange("p (c i) j -> p c j i", i=4),
                in_=held["raw", c][:, :, rest].rearrange("p j (c i) -> p c j i", i=4),
            )

        def square(c):
            if not is_chunk(c):
                return
            sq_grouped = wide.tile([P, CHUNKS[c] * PACK], BF16, align_bytes=64)
            nc.vector.tensor_mul(out=sq_grouped[:], in0=held["x", c], in1=held["x", c])
            held["sq", c] = sq_grouped[:]

        def quantise(what, c):
            if not is_chunk(c):
                return
            codes = wide.tile([P, CHUNKS[c]], U32, align_bytes=64, tag=what + "_codes")
            scales = wide.tile([P, CHUNKS[c]], U8, align_bytes=64, tag=what + "_scales")
            nc.vector.quantize_mx(out=codes[:].bitcast(FP8X4), scales=scales[:], in_=held[what, c])
            held[what + "_mx", c] = (codes, scales)

        def multiply(u):
            if not is_unit(u):
                return
            c, first, width = UNITS[u]
            cols = slice(first, first + width)
            acc = psum_mx.tile([P, width], F32)
            for w, what in enumerate(("sq_mx", "x_mx")):
                codes, scales = held[what, c]
                nc.tensor.matmul_mx(
                    out=acc[:],
                    lhsT=w_codes[:, w, :].bitcast(FP8X4),
                    lhsT_scale=w_scales[:, w, :],
                    rhs=codes[:, cols].bitcast(FP8X4),
                    rhs_scale=scales[:, cols],
                    start=(w == 0),
                    stop=(w == 1),
                )
            held["acc", u] = acc

        def blocks_of(u):
            return UNITS[u][2] // P

        def add_bias_and_transpose(u):
            if not is_unit(u):
                return
            logits = soft.tile([P, blocks_of(u), P], F32)
            nc.scalar.activation(
                out=logits[:].rearrange("k g n -> k (g n)"), in_=held["acc", u][:], func=ACT.Identity, bias=bias[:, 0:1]
            )
            logits_t = psum_t.tile([P, blocks_of(u), P], F32, tag="by_point")
            for g in range(blocks_of(u)):
                nc.tensor.transpose(logits_t[:, g, :], logits[:, g, :], ident[:])
            held["logits_t", u] = logits_t

        def find_max(u):
            if not is_unit(u):
                return
            neg_max = soft.tile([P, blocks_of(u)], F32)
            nc.vector.tensor_reduce(out=neg_max[:], in_=held["logits_t", u][:], axis=AXIS.X, op=ALU.max, negate=True)
            held["neg_max", u] = neg_max

        def exponentiate(u):
            if not is_unit(u):
                return
            expo = soft.tile([P, blocks_of(u), P], F32)
            total = soft.tile([P, blocks_of(u)], F32)
            for g in range(blocks_of(u)):
                nc.scalar.activation(
                    out=expo[:, g, :],
                    in_=held["logits_t", u][:, g, :],
                    func=ACT.Exp,
                    bias=held["neg_max", u][:, g : g + 1],
                    accum_out=total[:, g : g + 1],
                )
            held["expo", u] = expo
            held["total", u] = total

        def invert_total(u):
            if not is_unit(u):
                return
            inv_total = soft.tile([P, blocks_of(u)], F32)
            nc.vector.reciprocal(out=inv_total[:], in_=held["total", u][:])
            held["inv_total", u] = inv_total

        def normalise_and_transpose(u):
            if not is_unit(u):
                return
            prob = soft.tile([P, blocks_of(u), P], F32)
            for g in range(blocks_of(u)):
                nc.vector.tensor_scalar_mul(
                    out=prob[:, g, :], in0=held["expo", u][:, g, :], scalar1=held["inv_total", u][:, g : g + 1]
                )
            prob_t = psum_b.tile([P, blocks_of(u), P], F32)
            for g in range(blocks_of(u)):
                nc.tensor.transpose(prob_t[:, g, :], prob[:, g, :], ident[:])
            held["prob_t", u] = prob_t

        def store_out(u):
            if not is_unit(u):
                return
            c, first, width = UNITS[u]
            b, cols = hbm_cols(CHUNK_FIRSTS[c] + first, width)
            result = store.tile([P, width], F32)
            nc.scalar.copy(out=result[:], in_=held["prob_t", u][:].rearrange("k g n -> k (g n)"))
            nc.sync.dma_start(out=out[b, :, cols], in_=result[:])

        def front_steps(r):
            load_x(r + LOADS_AHEAD)
            quantise("sq", r - 1)
            group_on_scalar(r + 1)
            group_on_tensor(r + 1)
            quantise("x", r)

        def middle_steps(r):
            square(r)
            group_on_vector(r + 1)

        def back_steps(u):
            multiply(u)
            add_bias_and_transpose(u)
            invert_total(u - 4)
            find_max(u - 2)
            store_out(u - 5)
            exponentiate(u - 2)
            normalise_and_transpose(u - 4)

        ident = const.tile([P, P], F32)
        make_identity(nc, ident[:])
        ident_bf16 = const.tile([P, P], BF16)
        make_identity(nc, ident_bf16[:])
        mu_raw, mu2, log_sc, inv_s2 = start_clusters(nc, const, mu, sigma)
        for c in range(LOADS_AHEAD):
            load_x(c)
        group_on_scalar(0)
        group_on_tensor(0)
        group_on_vector(0)
        front_steps(0)
        middle_steps(0)
        w_grouped, bias = combine_clusters(nc, const, psum_t, mu_raw, mu2, log_sc, inv_s2)
        for r in range(1, len(CHUNKS) + 1):
            front_steps(r)
            if r == 1:
                w_codes, w_scales = quantise_clusters(nc, const, w_grouped)
            units = [u for u in range(len(UNITS)) if UNITS[u][0] == r - 1]
            half = (len(units) + 1) // 2
            for u in units[:half]:
                back_steps(u)
            middle_steps(r)
            for u in units[half:]:
                back_steps(u)
        for u in range(len(UNITS), len(UNITS) + 5):
            back_steps(u)
